import numpy as np
import ml_dtypes


def mxq(x, axis, fmt="e4m3"):
    dtype, down = {"e4m3": (ml_dtypes.float8_e4m3fn, 7), "e5m2": (ml_dtypes.float8_e5m2, 14)}[fmt]
    v = np.moveaxis(np.asarray(x, np.float32).astype(ml_dtypes.bfloat16).astype(np.float64), axis, -1)
    blocks = v.reshape(v.shape[:-1] + (-1, 32))
    amax = np.abs(blocks).max(-1, keepdims=True)
    byte = np.maximum(np.where(amax > 0, np.frexp(amax)[1] - 1 + 127, 0) - down, 1)
    scale = np.exp2(byte - 127.0)
    codes = (blocks / scale).astype(np.float32).astype(dtype).astype(np.float64)
    return np.moveaxis((codes * scale).reshape(v.shape), -1, axis)


WIDE = False


def mx_kscale(k):
    if not WIDE:
        return np.ones(k)
    levels = np.array([10, -10, 5, -5, 0])
    if k % 512:
        return np.exp2(np.random.permutation(np.resize(levels, k // 32))).repeat(32)
    a = np.empty((k // 512, 16))
    for p in range(k // 512):
        a[p, :8] = np.random.permutation(np.resize(levels, 8))
        for g in range(8):
            far = levels[np.abs(levels - a[p, g]) >= 10]
            a[p, g + 8] = far[np.random.randint(len(far))]
    return np.exp2(a.ravel()).repeat(32)


BF16 = ml_dtypes.bfloat16


def bf(x):
    return np.asarray(x, np.float32).astype(BF16)


def f64(x):
    return np.asarray(x).astype(np.float64)


E2M1 = np.array([0.0, 0.5, 1.0, 1.5, 2.0, 3.0, 4.0, 6.0, -0.0, -0.5, -1.0, -1.5, -2.0, -3.0, -4.0, -6.0])


def pack_weight(w, fmt):
    k, n = w.shape
    w = f64(bf(w)).reshape(k // 32, 32, n)
    amax = np.abs(w).max(1)
    if fmt == "e4m3":
        byte = np.frexp(amax)[1] - 1 + 127 - 7
    else:
        mant, ex = np.frexp(amax / 6.0)
        byte = np.where(mant > 0.5, ex, ex - 1) + 127
    byte = np.clip(np.where(amax > 0, byte, 1), 1, 254)
    scaled = (w * np.exp2(127.0 - byte)[:, None, :]).reshape(k, n).astype(np.float32)
    by_word = np.ascontiguousarray(scaled.reshape(k // 512, 128, 4, n).transpose(0, 1, 3, 2))
    if fmt == "e4m3":
        words = by_word.astype(ml_dtypes.float8_e4m3fn).view(np.uint8)
    else:
        c = by_word.astype(ml_dtypes.float4_e2m1fn).view(np.uint8) & 0xF
        words = c[..., 0::2] | (c[..., 1::2] << 4)
    return np.ascontiguousarray(words), np.ascontiguousarray(byte.astype(np.uint8).reshape(k // 512, 16, n))


def unpack_weight(words, scales, fmt):
    g, p, n, _ = words.shape
    if fmt == "e4m3":
        vals = np.ascontiguousarray(words).view(ml_dtypes.float8_e4m3fn).astype(np.float64)
    else:
        nib = np.empty((g, p, n, 4), np.uint8)
        nib[..., 0::2] = words & 0xF
        nib[..., 1::2] = words >> 4
        vals = E2M1[nib]
    vals = vals * np.repeat(np.exp2(scales.astype(np.float64) - 127.0), 8, axis=1)[..., None]
    return vals.transpose(0, 1, 3, 2).reshape(g * 512, n)
def pack4(w):
    words, scales = pack_weight(w, "e2m1")
    return words.reshape(words.shape[0], 128, -1), scales


def unpack4(words, scales):
    return unpack_weight(words.reshape(words.shape[0], 128, -1, 2), scales, "e2m1")


B, DIM, DI, H, W = 4, 512, 512, 32, 16
N = H * W
EPS = 1e-5
A = 2.0


def draw0():
    s, t = mx_kscale(DI), mx_kscale(DI)
    attention = bf(np.random.standard_normal((B, DI, DI)) * A * A * np.sqrt(N) / DI * t[None, :, None] * s[None, None, :])
    g_x = bf(np.random.standard_normal((B, DI, N)) / s[None, :, None])
    x = bf(np.random.standard_normal((B, DIM, H, W)))
    Ww = np.random.standard_normal((DIM, DI)) * 0.5 / np.sqrt(DI) / t[None, :]
    Ww_words, Ww_scales = pack4(Ww.T)
    return {"attention": attention,
            "g_x": g_x,
            "x": x,
            "Ww_words": Ww_words,
            "Ww_scales": Ww_scales,
            "bw": bf(np.random.standard_normal(DIM) * 0.5),
            "gamma": bf(np.random.standard_normal(DIM) * 0.3),
            "beta": bf(np.random.standard_normal(DIM) * 0.3),
            "run_mean": bf(np.random.standard_normal(DIM) * 0.5),
            "run_var": bf(np.random.uniform(0.5, 1.5, DIM))}


def core(attention, g_x, x, Ww_words, Ww_scales, bw, gamma, beta, run_mean, run_var):
    y = mxq(f64(attention), 2, "e4m3") @ mxq(f64(g_x), 1, "e4m3")
    W_y = (unpack4(Ww_words, Ww_scales).T @ mxq(y, 1, "e4m3")) + f64(bw)[None, :, None]
    inv = f64(gamma) / np.sqrt(f64(run_var) + EPS)
    W_y = (W_y - f64(run_mean)[None, :, None]) * inv[None, :, None] + f64(beta)[None, :, None]
    return W_y.reshape(B, DIM, H, W) + f64(x)


def e4m3fn_bytes(y):
    return np.clip(np.asarray(y, np.float64), -448.0, 448.0).astype(np.float32).astype(ml_dtypes.float8_e4m3fn).view(np.uint8)


def e4m3fn_values(b):
    return np.asarray(b, np.uint8).view(ml_dtypes.float8_e4m3fn).astype(np.float64)


def setup_inputs():
    d = draw0()
    x0 = np.asarray(d['g_x']).astype(np.float64)
    s = (np.max(np.abs(x0), axis=(0, 2), keepdims=True) / 448.0).astype(np.float32)
    out = {}
    for k, v in d.items():
        if k == 'g_x':
            out['g_x_bytes'] = e4m3fn_bytes(x0 / s.astype(np.float64))
            out['g_x_scale'] = s
        else:
            out[k] = v
    return out


def reference(attention, g_x_bytes, g_x_scale, x, Ww_words, Ww_scales, bw, gamma, beta, run_mean, run_var):
    return core(attention, e4m3fn_values(g_x_bytes) * g_x_scale.astype(np.float64), x, Ww_words, Ww_scales, bw, gamma, beta, run_mean, run_var)

@@ -1,0 +1,303 @@
+from contextlib import ExitStack
+
+import concourse.mybir as mybir
+from concourse.masks import make_identity
+
+F32 = mybir.dt.float32
+BF16 = mybir.dt.bfloat16
+I32 = mybir.dt.int32
+U32 = mybir.dt.uint32
+U8 = mybir.dt.uint8
+FP8 = mybir.dt.float8_e4m3fn
+FP8X4 = mybir.dt.float8_e4m3fn_x4
+FP4X4 = mybir.dt.float4_e2m1fn_x4
+ADD = mybir.AluOpType.add
+SUB = mybir.AluOpType.subtract
+MULT = mybir.AluOpType.mult
+POW = mybir.AluOpType.pow
+COPY = mybir.ActivationFunctionType.Copy
+
+P = 128
+B = 4
+C = 512
+N = 512
+EPS = 1e-5
+FLOPS = 2 * (2 * B * C * C * N)
+
+
+def tile_cnl_pb_w4_kernel(
+    tc, attention, g_x_bytes, g_x_scale, x, Ww_words, Ww_scales, bw, gamma, beta, run_mean, run_var, out
+):
+    nc = tc.nc
+    with ExitStack() as ctx:
+        keep = ctx.enter_context(tc.tile_pool(name="keep", bufs=1))
+        per = ctx.enter_context(tc.tile_pool(name="per", bufs=B))
+        psum = ctx.enter_context(tc.psum_pool(name="psum", bufs=3))
+        ctx.enter_context(tc.manual_schedule())
+
+        ident = keep.tile([P, P], F32)
+        make_identity(nc, ident[:])
+        ws_raw = keep.tile([P, C], U8, align_bytes=64)
+        nc.gpsimd.memset(ws_raw[:].bitcast(I32), 0)
+        prm = keep.tile([P, 5, 16], BF16)
+        for i, v in enumerate((run_var, gamma, bw, run_mean, beta)):
+            nc.gpsimd.dma_start(out=prm[:, i, 0:4], in_=v.rearrange("(p m) -> p m", m=4))
+        gsc = keep.tile([P, 4], F32)
+        nc.scalar.dma_start(out=gsc[:], in_=g_x_scale.rearrange("o (p t) u -> p (o t u)", t=4))
+
+        gb, ab, xb = [], [], []
+        for b in range(B):
+            g_bytes = per.tile([P, 4, N], U8, align_bytes=64)
+            gb.append(g_bytes)
+            a_raw = per.tile([P, 4, C], BF16, align_bytes=64)
+            ab.append(a_raw)
+            x_raw = per.tile([P, 4, N], BF16, align_bytes=64)
+            xb.append(x_raw)
+
+        def load_g(b):
+            nc.sync.dma_start(out=gb[b][:], in_=g_x_bytes[b].rearrange("(p t) n -> p t n", t=4))
+
+        def load_a(b, t0, t1):
+            nc.sync.dma_start(
+                out=ab[b][:, t0:t1, :], in_=attention[b].rearrange("(p t) k -> p t k", t=4)[:, t0:t1, :]
+            )
+
+        def load_x(b):
+            nc.sync.dma_start(out=xb[b][:], in_=x[b].rearrange("(p m) h w -> p m (h w)", m=4))
+
+        w_raw = keep.tile([P, 2 * C], U8, align_bytes=64)
+        load_g(0)
+        load_a(0, 0, 2)
+        load_a(0, 2, 4)
+        load_g(1)
+        load_a(1, 0, 4)
+        nc.sync.dma_start(out=w_raw[:], in_=Ww_words[0])
+        load_x(0)
+        for r in range(4):
+            nc.sync.dma_start(
+                out=ws_raw[32 * r : 32 * r + 4, :].bitcast(I32), in_=Ww_scales[0, 4 * r : 4 * r + 4, :].bitcast(I32)
+            )
+        load_g(2)
+        load_a(2, 0, 4)
+        load_x(1)
+        load_g(3)
+        load_a(3, 0, 4)
+        load_x(2)
+        load_x(3)
+
+        negh = keep.tile([P, 4], F32)
+        nc.gpsimd.memset(negh[:], -0.5)
+        ve = keep.tile([P, 4], F32)
+        inv = keep.tile([P, 4], F32)
+        bias = keep.tile([P, 4], F32)
+        rs = keep.tile([P, 4], F32)
+        dm = keep.tile([P, 4], F32)
+        de = keep.tile([P, 4], F32)
+        nc.gpsimd.tensor_scalar(out=ve[:], in0=prm[:, 0, 0:4], scalar1=EPS, scalar2=None, op0=ADD)
+        nc.gpsimd.tensor_tensor(out=rs[:], in0=ve[:], in1=negh[:], op=POW)
+        nc.gpsimd.tensor_tensor(out=inv[:], in0=rs[:], in1=prm[:, 1, 0:4], op=MULT)
+        nc.gpsimd.tensor_tensor(out=dm[:], in0=prm[:, 2, 0:4], in1=prm[:, 3, 0:4], op=SUB)
+        nc.gpsimd.tensor_tensor(out=de[:], in0=dm[:], in1=inv[:], op=MULT)
+        nc.gpsimd.tensor_tensor(out=bias[:], in0=de[:], in1=prm[:, 4, 0:4], op=ADD)
+
+        gp, gi, gc, gs, ai, ac, asc, yi, yc, ys, xp, ot = ([] for i in range(12))
+        for b in range(B):
+            g_planes = per.tile([P, 4, N], BF16, align_bytes=64)
+            gp.append(g_planes)
+            g_inter = per.tile([P, 4 * N], BF16, align_bytes=64)
+            gi.append(g_inter)
+            g_codes = per.tile([P, N], U32, align_bytes=64)
+            gc.append(g_codes)
+            g_scales = per.tile([P, N], U8, align_bytes=64)
+            gs.append(g_scales)
+            a_inter = per.tile([P, 4 * C], BF16, align_bytes=64)
+            ai.append(a_inter)
+            a_codes = per.tile([P, C], U32, align_bytes=64)
+            ac.append(a_codes)
+            a_scales = per.tile([P, C], U8, align_bytes=64)
+            asc.append(a_scales)
+            y_inter = per.tile([P, 4 * N], BF16, align_bytes=64)
+            yi.append(y_inter)
+            y_codes = per.tile([P, N], U32, align_bytes=64)
+            yc.append(y_codes)
+            y_scales = per.tile([P, N], U8, align_bytes=64)
+            ys.append(y_scales)
+            x_plus = per.tile([P, 4, N], F32, align_bytes=64)
+            xp.append(x_plus)
+            o_tile = per.tile([P, 4, N], F32, align_bytes=64)
+            ot.append(o_tile)
+        w_perm = keep.tile([P, 4, P, 2], U8, align_bytes=64)
+        ws_perm = keep.tile([P, 4, P], U8, align_bytes=64)
+
+        for b in range(B):
+            for m in range(4):
+                nc.gpsimd.tensor_scalar(
+                    out=xp[b][:, m, :], in0=xb[b][:, m, :], scalar1=1.0, scalar2=bias[:, m : m + 1], op0=MULT, op1=ADD
+                )
+
+        def widen_s(b, *planes):
+            for t in planes:
+                nc.scalar.activation(
+                    out=gp[b][:, t, :], in_=gb[b][:, t, :].bitcast(FP8), func=COPY, scale=gsc[:, t : t + 1]
+                )
+
+        def widen_v(b, *planes):
+            for t in planes:
+                nc.vector.tensor_scalar(
+                    out=gp[b][:, t, :], in0=gb[b][:, t, :].bitcast(FP8), scalar1=gsc[:, t : t + 1], scalar2=None, op0=MULT
+                )
+
+        def inter(b, h):
+            n0, n1 = h * 256, (h + 1) * 256
+            nc.vector.tensor_copy(
+                out=gi[b][:, 4 * n0 : 4 * n1].rearrange("p (c i t) -> p c t i", i=4, t=4),
+                in_=gp[b][:, :, n0:n1].rearrange("p t (c i) -> p c t i", i=4),
+            )
+
+        def quant(src, codes, scales, c0, c1):
+            nc.vector.quantize_mx(
+                out=codes[:, c0:c1].bitcast(FP8X4), scales=scales[:, c0:c1], in_=src[:, 4 * c0 : 4 * c1]
+            )
+
+        def qg(b, c0, c1):
+            quant(gi[b], gc[b], gs[b], c0, c1)
+
+        def qa(b):
+            quant(ai[b], ac[b], asc[b], 0, C)
+
+        def qy(b, h):
+            quant(yi[b], yc[b], ys[b], 256 * h, 256 * h + 256)
+
+        xts = {}
+
+        def turn(b, h):
+            xt = psum.tile([P, 2, 2, P], F32, bufs=2)
+            for i in range(2):
+                words = ab[b][:, 2 * h + i, :].bitcast(F32)
+                for u in range(2):
+                    nc.tensor.transpose(xt[:, i, u, :], words[:, u : C // 2 : 2], ident[:])
+            xts[(b, h)] = xt
+
+        def acopy(b, h):
+            nc.scalar.copy(
+                out=ai[b][:, 1024 * h : 1024 * h + 1024].bitcast(F32).rearrange("p (i m u) -> p i m u", i=2, u=2),
+                in_=xts[(b, h)][:].rearrange("p i u m -> p i m u"),
+            )
+
+        yps = {}
+
+        def m1(b, j):
+            yp = psum.tile([P, 4, P], F32, bufs=3)
+            for t in range(4):
+                nc.tensor.matmul_mx(
+                    out=yp[:, t, :],
+                    lhsT=ac[b][:, t * P : t * P + P].bitcast(FP8X4),
+                    lhsT_scale=asc[b][:, t * P : t * P + P],
+                    rhs=gc[b][:, j * P : j * P + P].bitcast(FP8X4),
+                    rhs_scale=gs[b][:, j * P : j * P + P],
+                    start=True,
+                    stop=True,
+                )
+            yps[(b, j)] = yp
+
+        def ycopy(b, *js):
+            for j in js:
+                nc.scalar.copy(
+                    out=yi[b][:, 512 * j : 512 * j + 512].rearrange("p (n t) -> p n t", t=4),
+                    in_=yps[(b, j)][:].rearrange("p t n -> p n t"),
+                )
+
+        zps = {}
+
+        def m2(b, m, n0, n1):
+            zp = psum.tile([P, n1 - n0], F32, bufs=3)
+            nc.tensor.matmul_mx(
+                out=zp[:],
+                lhsT=w_perm[:, m, :, :].rearrange("p q b -> p (q b)").bitcast(FP4X4),
+                lhsT_scale=ws_perm[:, m, :],
+                rhs=yc[b][:, n0:n1].bitcast(FP8X4),
+                rhs_scale=ys[b][:, n0:n1],
+                start=True,
+                stop=True,
+            )
+            zps[(b, m, n0)] = zp
+
+        def fin(b, m, n0, n1):
+            nc.vector.scalar_tensor_tensor(
+                out=ot[b][:, m, n0:n1],
+                in0=zps[(b, m, n0)][:],
+                scalar=inv[:, m : m + 1],
+                in1=xp[b][:, m, n0:n1],
+                op0=MULT,
+                op1=ADD,
+            )
+
+        def store(b, m0, m1_, n0, n1):
+            nc.sync.dma_start(
+                out=out[b].rearrange("(p m) h w -> p m (h w)", m=4)[:, m0:m1_, n0:n1], in_=ot[b][:, m0:m1_, n0:n1]
+            )
+
+        def m1y(b, *js):
+            for j in js:
+                m1(b, j)
+                ycopy(b, j)
+
+        def m2fin(b, *ms):
+            for m in ms:
+                m2(b, m, 0, N)
+                fin(b, m, 0, N)
+                if m % 2 == 1:
+                    store(b, m - 1, m + 1, 0, N)
+
+        turn(0, 0)
+        turn(0, 1)
+        widen_s(0, 0)
+        widen_v(0, 1, 2, 3)
+        inter(0, 0)
+        qg(0, 0, 256)
+        acopy(0, 0)
+        acopy(0, 1)
+        inter(0, 1)
+        qa(0)
+        qg(0, 256, 512)
+        widen_s(1, 0, 1, 2, 3)
+        turn(1, 0)
+        turn(1, 1)
+        acopy(1, 0)
+        acopy(1, 1)
+        nc.vector.tensor_copy(out=w_perm[:], in_=w_raw[:].rearrange("p (q m b) -> p m q b", m=4, b=2))
+        inter(1, 0)
+        inter(1, 1)
+        qg(1, 0, 512)
+        qa(1)
+        m1y(0, 0, 1, 2, 3)
+        nc.vector.tensor_copy(out=ws_perm[:], in_=ws_raw[:].rearrange("p (q m) -> p m q", m=4))
+        qy(0, 0)
+        qy(0, 1)
+        for b in range(2):
+            turn(b + 2, 0)
+            turn(b + 2, 1)
+            widen_s(b + 2, 0, 1, 2, 3)
+            acopy(b + 2, 0)
+            acopy(b + 2, 1)
+            m2fin(b, 0, 1, 2, 3)
+            inter(b + 2, 0)
+            inter(b + 2, 1)
+            qg(b + 2, 0, 512)
+            m1y(b + 1, 0, 1)
+            qy(b + 1, 0)
+            qa(b + 2)
+            m1y(b + 1, 2, 3)
+            qy(b + 1, 1)
+        m1y(3, 0, 1)
+        m2fin(2, 0, 1)
+        m1y(3, 2, 3)
+        qy(3, 0)
+        m2fin(2, 2, 3)
+        for h in range(2):
+            if h == 1:
+                qy(3, 1)
+            for m in range(4):
+                m2(3, m, 256 * h, 256 * h + 256)
+                fin(3, m, 256 * h, 256 * h + 256)
+            store(3, 0, 4, 256 * h, 256 * h + 256)

@@ -39,9 +39,10 @@ def tile_cnl_pb_w4_kernel(
         make_identity(nc, ident[:])
         ws_raw = keep.tile([P, C], U8, align_bytes=64)
         nc.gpsimd.memset(ws_raw[:].bitcast(I32), 0)
-        prm = keep.tile([P, 5, 16], BF16)
+        rows = keep.tile([P, C], BF16, align_bytes=64)
+        nc.gpsimd.memset(rows[:].bitcast(I32), 0)
         for i, v in enumerate((run_var, gamma, bw, run_mean, beta)):
-            nc.gpsimd.dma_start(out=prm[:, i, 0:4], in_=v.rearrange("(p m) -> p m", m=4))
+            nc.gpsimd.dma_start(out=rows[i : i + 1, :], in_=v.rearrange("(o c) -> o c", o=1))
         gsc = keep.tile([P, 4], F32)
         nc.scalar.dma_start(out=gsc[:], in_=g_x_scale.rearrange("o (p t) u -> p (o t u)", t=4))
 
@@ -63,7 +64,7 @@ def tile_cnl_pb_w4_kernel(
             )
 
         def load_x(b):
-            nc.sync.dma_start(out=xb[b][:], in_=x[b].rearrange("(p m) h w -> p m (h w)", m=4))
+            nc.sync.dma_start(out=xb[b][:], in_=x[b].rearrange("(m p) h w -> p m (h w)", m=4))
 
         w_raw = keep.tile([P, 2 * C], U8, align_bytes=64)
         load_g(0)
@@ -87,20 +88,30 @@ def tile_cnl_pb_w4_kernel(
 
         negh = keep.tile([P, 4], F32)
         nc.gpsimd.memset(negh[:], -0.5)
+        prm = keep.tile([P, 5, 4], F32)
         ve = keep.tile([P, 4], F32)
         inv = keep.tile([P, 4], F32)
         bias = keep.tile([P, 4], F32)
         rs = keep.tile([P, 4], F32)
         dm = keep.tile([P, 4], F32)
         de = keep.tile([P, 4], F32)
-        nc.gpsimd.tensor_scalar(out=ve[:], in0=prm[:, 0, 0:4], scalar1=EPS, scalar2=None, op0=ADD)
-        nc.gpsimd.tensor_tensor(out=rs[:], in0=ve[:], in1=negh[:], op=POW)
-        nc.gpsimd.tensor_tensor(out=inv[:], in0=rs[:], in1=prm[:, 1, 0:4], op=MULT)
-        nc.gpsimd.tensor_tensor(out=dm[:], in0=prm[:, 2, 0:4], in1=prm[:, 3, 0:4], op=SUB)
-        nc.gpsimd.tensor_tensor(out=de[:], in0=dm[:], in1=inv[:], op=MULT)
-        nc.gpsimd.tensor_tensor(out=bias[:], in0=de[:], in1=prm[:, 4, 0:4], op=ADD)
+        ident_bf = keep.tile([P, P], BF16)
+        nc.vector.tensor_copy(out=ident_bf[:], in_=ident[:])
 
-        gp, gi, gc, gs, ai, ac, asc, yi, yc, ys, xp, ot = ([] for i in range(12))
+        def params():
+            pt = psum.tile([P, 4, P], BF16, tag="zp", bufs=3)
+            for m in range(4):
+                nc.tensor.transpose(pt[:, m, :], rows[:, m * P : m * P + P], ident_bf[:])
+            nc.vector.tensor_copy(out=prm[:].rearrange("p i m -> p m i"), in_=pt[:, :, 0:5])
+            nc.gpsimd.tensor_scalar(out=ve[:], in0=prm[:, 0, :], scalar1=EPS, scalar2=None, op0=ADD)
+            nc.gpsimd.tensor_tensor(out=rs[:], in0=ve[:], in1=negh[:], op=POW)
+            nc.gpsimd.tensor_tensor(out=inv[:], in0=rs[:], in1=prm[:, 1, :], op=MULT)
+            nc.gpsimd.tensor_tensor(out=dm[:], in0=prm[:, 2, :], in1=prm[:, 3, :], op=SUB)
+            nc.gpsimd.tensor_tensor(out=de[:], in0=dm[:], in1=inv[:], op=MULT)
+            nc.gpsimd.tensor_tensor(out=bias[:], in0=de[:], in1=prm[:, 4, :], op=ADD)
+
+        gp, gi, gc, gs, ai, ac, asc, yi, yc, ys, ot = ([] for i in range(11))
+        xp = {}
         for b in range(B):
             g_planes = per.tile([P, 4, N], BF16, align_bytes=64)
             gp.append(g_planes)
@@ -122,18 +133,15 @@ def tile_cnl_pb_w4_kernel(
             yc.append(y_codes)
             y_scales = per.tile([P, N], U8, align_bytes=64)
             ys.append(y_scales)
-            x_plus = per.tile([P, 4, N], F32, align_bytes=64)
-            xp.append(x_plus)
             o_tile = per.tile([P, 4, N], F32, align_bytes=64)
             ot.append(o_tile)
-        w_perm = keep.tile([P, 4, P, 2], U8, align_bytes=64)
-        ws_perm = keep.tile([P, 4, P], U8, align_bytes=64)
 
-        for b in range(B):
-            for m in range(4):
-                nc.gpsimd.tensor_scalar(
-                    out=xp[b][:, m, :], in0=xb[b][:, m, :], scalar1=1.0, scalar2=bias[:, m : m + 1], op0=MULT, op1=ADD
-                )
+        def addb(b, m):
+            x_plus = keep.tile([P, N], F32, align_bytes=64, name="x_plus_%d_%d" % (b, m), tag="x_plus_%d" % m)
+            xp[(b, m)] = x_plus
+            nc.gpsimd.tensor_scalar(
+                out=x_plus[:], in0=xb[b][:, m, :], scalar1=1.0, scalar2=bias[:, m : m + 1], op0=MULT, op1=ADD
+            )
 
         def widen_s(b, *planes):
             for t in planes:
@@ -210,11 +218,11 @@ def tile_cnl_pb_w4_kernel(
         zps = {}
 
         def m2(b, m, n0, n1):
-            zp = psum.tile([P, n1 - n0], F32, bufs=3)
+            zp = psum.tile([P, n1 - n0], F32, tag="zp", bufs=3)
             nc.tensor.matmul_mx(
                 out=zp[:],
-                lhsT=w_perm[:, m, :, :].rearrange("p q b -> p (q b)").bitcast(FP4X4),
-                lhsT_scale=ws_perm[:, m, :],
+                lhsT=w_raw[:, 2 * P * m : 2 * P * m + 2 * P].bitcast(FP4X4),
+                lhsT_scale=ws_raw[:, P * m : P * m + P],
                 rhs=yc[b][:, n0:n1].bitcast(FP8X4),
                 rhs_scale=ys[b][:, n0:n1],
                 start=True,
@@ -227,25 +235,26 @@ def tile_cnl_pb_w4_kernel(
                 out=ot[b][:, m, n0:n1],
                 in0=zps[(b, m, n0)][:],
                 scalar=inv[:, m : m + 1],
-                in1=xp[b][:, m, n0:n1],
+                in1=xp[(b, m)][:, n0:n1],
                 op0=MULT,
                 op1=ADD,
             )
 
         def store(b, m0, m1_, n0, n1):
             nc.sync.dma_start(
-                out=out[b].rearrange("(p m) h w -> p m (h w)", m=4)[:, m0:m1_, n0:n1], in_=ot[b][:, m0:m1_, n0:n1]
+                out=out[b].rearrange("(m p) h w -> p m (h w)", m=4)[:, m0:m1_, n0:n1], in_=ot[b][:, m0:m1_, n0:n1]
             )
 
-        def m1y(b, *js):
+        def m1s(b, *js):
             for j in js:
                 m1(b, j)
-                ycopy(b, j)
 
         def m2fin(b, *ms):
             for m in ms:
                 m2(b, m, 0, N)
                 fin(b, m, 0, N)
+                if b + 1 < B:
+                    addb(b + 1, m)
                 if m % 2 == 1:
                     store(b, m - 1, m + 1, 0, N)
 
@@ -254,50 +263,70 @@ def tile_cnl_pb_w4_kernel(
         widen_s(0, 0)
         widen_v(0, 1, 2, 3)
         inter(0, 0)
-        qg(0, 0, 256)
         acopy(0, 0)
         acopy(0, 1)
         inter(0, 1)
+        qg(0, 0, 256)
         qa(0)
         qg(0, 256, 512)
-        widen_s(1, 0, 1, 2, 3)
         turn(1, 0)
         turn(1, 1)
+        widen_v(1, 0, 1)
+        widen_s(1, 2, 3)
         acopy(1, 0)
         acopy(1, 1)
-        nc.vector.tensor_copy(out=w_perm[:], in_=w_raw[:].rearrange("p (q m b) -> p m q b", m=4, b=2))
         inter(1, 0)
         inter(1, 1)
-        qg(1, 0, 512)
+        m1s(0, 0, 1, 2, 3)
+        params()
+        for m in range(4):
+            addb(0, m)
         qa(1)
-        m1y(0, 0, 1, 2, 3)
-        nc.vector.tensor_copy(out=ws_perm[:], in_=ws_raw[:].rearrange("p (q m) -> p m q", m=4))
+        ycopy(0, 0, 1, 2, 3)
         qy(0, 0)
+        qg(1, 0, 512)
         qy(0, 1)
-        for b in range(2):
-            turn(b + 2, 0)
-            turn(b + 2, 1)
-            widen_s(b + 2, 0, 1, 2, 3)
-            acopy(b + 2, 0)
-            acopy(b + 2, 1)
-            m2fin(b, 0, 1, 2, 3)
-            inter(b + 2, 0)
-            inter(b + 2, 1)
-            qg(b + 2, 0, 512)
-            m1y(b + 1, 0, 1)
-            qy(b + 1, 0)
-            qa(b + 2)
-            m1y(b + 1, 2, 3)
-            qy(b + 1, 1)
-        m1y(3, 0, 1)
+        m1s(1, 0, 1)
+        widen_s(2, 0, 1, 2, 3)
+        m2fin(0, 0, 1, 2, 3)
+        m1s(1, 2, 3)
+        turn(2, 0)
+        turn(2, 1)
+        ycopy(1, 0, 1, 2, 3)
+        inter(2, 0)
+        qy(1, 0)
+        inter(2, 1)
+        qy(1, 1)
+        qg(2, 0, 512)
+        acopy(2, 0)
+        acopy(2, 1)
+        widen_s(3, 0, 1, 2, 3)
+        m2fin(1, 0, 1, 2, 3)
+        turn(3, 0)
+        turn(3, 1)
+        acopy(3, 0)
+        acopy(3, 1)
+        qa(2)
+        inter(3, 0)
+        m1s(2, 0, 1, 2, 3)
+        ycopy(2, 0, 1, 2, 3)
+        inter(3, 1)
+        qa(3)
+        qg(3, 0, 512)
+        qy(2, 0)
+        qy(2, 1)
+        m1s(3, 0, 1)
+        ycopy(3, 0, 1)
         m2fin(2, 0, 1)
-        m1y(3, 2, 3)
+        m1s(3, 2, 3)
+        ycopy(3, 2, 3)
         qy(3, 0)
         m2fin(2, 2, 3)
         for h in range(2):
-            if h == 1:
+            if h == 0:
                 qy(3, 1)
             for m in range(4):
                 m2(3, m, 256 * h, 256 * h + 256)
                 fin(3, m, 256 * h, 256 * h + 256)
-            store(3, 0, 4, 256 * h, 256 * h + 256)
+                if m % 2 == 1:
+                    store(3, m - 1, m + 1, 256 * h, 256 * h + 256)

@@ -38,13 +38,10 @@ def tile_cnl_pb_w4_kernel(
         ident = keep.tile([P, P], F32)
         make_identity(nc, ident[:])
         ws_raw = keep.tile([P, C], U8, align_bytes=64)
-        nc.gpsimd.memset(ws_raw[:].bitcast(I32), 0)
         rows = keep.tile([P, C], BF16, align_bytes=64)
-        nc.gpsimd.memset(rows[:].bitcast(I32), 0)
-        for i, v in enumerate((run_var, gamma, bw, run_mean, beta)):
-            nc.gpsimd.dma_start(out=rows[i : i + 1, :], in_=v.rearrange("(o c) -> o c", o=1))
+        nc.vector.memset(rows[:].bitcast(I32), 0)
+        nc.vector.memset(ws_raw[:].bitcast(I32), 0)
         gsc = keep.tile([P, 4], F32)
-        nc.scalar.dma_start(out=gsc[:], in_=g_x_scale.rearrange("o (p t) u -> p (o t u)", t=4))
 
         gb, ab, xb = [], [], []
         for b in range(B):
@@ -68,8 +65,10 @@ def tile_cnl_pb_w4_kernel(
 
         w_raw = keep.tile([P, 2 * C], U8, align_bytes=64)
         load_g(0)
-        load_a(0, 0, 2)
-        load_a(0, 2, 4)
+        load_a(0, 0, 4)
+        nc.scalar.dma_start(out=gsc[:], in_=g_x_scale.rearrange("o (p t) u -> p (o t u)", t=4))
+        for i, v in enumerate((run_var, gamma, bw, run_mean, beta)):
+            nc.scalar.dma_start(out=rows[i : i + 1, :], in_=v.rearrange("(o c) -> o c", o=1))
         load_g(1)
         load_a(1, 0, 4)
         nc.sync.dma_start(out=w_raw[:], in_=Ww_words[0])
@@ -258,10 +257,13 @@ def tile_cnl_pb_w4_kernel(
                 if m % 2 == 1:
                     store(b, m - 1, m + 1, 0, N)
 
+        widen_s(0, 0, 1)
+        widen_v(0, 2, 3)
+        params()
+        for m in range(4):
+            addb(0, m)
         turn(0, 0)
         turn(0, 1)
-        widen_s(0, 0)
-        widen_v(0, 1, 2, 3)
         inter(0, 0)
         acopy(0, 0)
         acopy(0, 1)
@@ -278,9 +280,6 @@ def tile_cnl_pb_w4_kernel(
         inter(1, 0)
         inter(1, 1)
         m1s(0, 0, 1, 2, 3)
-        params()
-        for m in range(4):
-            addb(0, m)
         qa(1)
         ycopy(0, 0, 1, 2, 3)
         qy(0, 0)

@@ -16,6 +16,7 @@ SUB = mybir.AluOpType.subtract
 MULT = mybir.AluOpType.mult
 POW = mybir.AluOpType.pow
 COPY = mybir.ActivationFunctionType.Copy
+IDENT = mybir.ActivationFunctionType.Identity
 
 P = 128
 B = 4
@@ -97,10 +98,16 @@ def tile_cnl_pb_w4_kernel(
         ident_bf = keep.tile([P, P], BF16)
         nc.vector.tensor_copy(out=ident_bf[:], in_=ident[:])
 
-        def params():
+        pts = []
+
+        def params_turn():
             pt = psum.tile([P, 4, P], BF16, tag="zp", bufs=3)
             for m in range(4):
                 nc.tensor.transpose(pt[:, m, :], rows[:, m * P : m * P + P], ident_bf[:])
+            pts.append(pt)
+
+        def params():
+            pt = pts[0]
             nc.vector.tensor_copy(out=prm[:].rearrange("p i m -> p m i"), in_=pt[:, :, 0:5])
             nc.gpsimd.tensor_scalar(out=ve[:], in0=prm[:, 0, :], scalar1=EPS, scalar2=None, op0=ADD)
             nc.gpsimd.tensor_tensor(out=rs[:], in0=ve[:], in1=negh[:], op=POW)
@@ -135,12 +142,39 @@ def tile_cnl_pb_w4_kernel(
             o_tile = per.tile([P, 4, N], F32, align_bytes=64)
             ot.append(o_tile)
 
-        def addb(b, m):
-            x_plus = keep.tile([P, N], F32, align_bytes=64, name="x_plus_%d_%d" % (b, m), tag="x_plus_%d" % m)
-            xp[(b, m)] = x_plus
-            nc.gpsimd.tensor_scalar(
-                out=x_plus[:], in0=xb[b][:, m, :], scalar1=1.0, scalar2=bias[:, m : m + 1], op0=MULT, op1=ADD
+        gates = {}
+
+        def gate(b):
+            gated = per.tile([P, 4], F32)
+            nc.vector.tensor_copy(out=gated[:], in_=bias[:])
+            gates[b] = gated
+
+        def addb(engine, b, *ms):
+            for m in ms:
+                x_plus = keep.tile([P, N], F32, align_bytes=64, name="x_plus_%d_%d" % (b, m), tag="x_plus_%d" % m, bufs=2)
+                xp[(b, m)] = x_plus
+                if engine == "s":
+                    nc.scalar.activation(out=x_plus[:], in_=xb[b][:, m, :], func=IDENT, bias=bias[:, m : m + 1])
+                elif engine == "v":
+                    nc.vector.tensor_scalar(
+                        out=x_plus[:], in0=xb[b][:, m, :], scalar1=bias[:, m : m + 1], scalar2=None, op0=ADD
+                    )
+                else:
+                    nc.gpsimd.tensor_scalar(
+                        out=x_plus[:],
+                        in0=xb[b][:, m, :],
+                        scalar1=1.0,
+                        scalar2=gates[b][:, m : m + 1],
+                        op0=MULT,
+                        op1=ADD,
+                    )
+
+        def fin_sg(b, m):
+            scaled = keep.tile([P, N], F32, align_bytes=64, bufs=2)
+            nc.scalar.activation(
+                out=scaled[:], in_=zps[(b, m, 0)][:], func=IDENT, bias=bias[:, m : m + 1], scale=inv[:, m : m + 1]
             )
+            nc.gpsimd.tensor_tensor(out=ot[b][:, m, :], in0=scaled[:], in1=xb[b][:, m, :], op=ADD)
 
         def widen_s(b, *planes):
             for t in planes:
@@ -252,28 +286,27 @@ def tile_cnl_pb_w4_kernel(
             for m in ms:
                 m2(b, m, 0, N)
                 fin(b, m, 0, N)
-                if b + 1 < B:
-                    addb(b + 1, m)
-                if m % 2 == 1:
+                if b >= 2:
+                    store(b, m, m + 1, 0, N)
+                elif m % 2 == 1:
                     store(b, m - 1, m + 1, 0, N)
 
-        widen_s(0, 0, 1)
-        widen_v(0, 2, 3)
-        params()
-        for m in range(4):
-            addb(0, m)
+        widen_s(0, 0)
+        widen_v(0, 1, 2, 3)
+        params_turn()
         turn(0, 0)
         turn(0, 1)
         inter(0, 0)
         acopy(0, 0)
         acopy(0, 1)
         inter(0, 1)
+        params()
         qg(0, 0, 256)
+        widen_v(1, 0, 1)
         qa(0)
         qg(0, 256, 512)
         turn(1, 0)
         turn(1, 1)
-        widen_v(1, 0, 1)
         widen_s(1, 2, 3)
         acopy(1, 0)
         acopy(1, 1)
@@ -286,6 +319,10 @@ def tile_cnl_pb_w4_kernel(
         qg(1, 0, 512)
         qy(0, 1)
         m1s(1, 0, 1)
+        addb("v", 0, 2, 3)
+        addb("s", 0, 0, 1)
+        gate(1)
+        addb("g", 1, 0, 1, 2, 3)
         widen_s(2, 0, 1, 2, 3)
         m2fin(0, 0, 1, 2, 3)
         m1s(1, 2, 3)
@@ -300,6 +337,8 @@ def tile_cnl_pb_w4_kernel(
         acopy(2, 0)
         acopy(2, 1)
         widen_s(3, 0, 1, 2, 3)
+        gate(2)
+        addb("g", 2, 0, 1, 2, 3)
         m2fin(1, 0, 1, 2, 3)
         turn(3, 0)
         turn(3, 1)
@@ -311,21 +350,29 @@ def tile_cnl_pb_w4_kernel(
         ycopy(2, 0, 1, 2, 3)
         inter(3, 1)
         qa(3)
-        qg(3, 0, 512)
+        qg(3, 0, 256)
+        m1s(3, 0, 1)
         qy(2, 0)
         qy(2, 1)
-        m1s(3, 0, 1)
+        qg(3, 256, 512)
         ycopy(3, 0, 1)
+        gate(3)
+        addb("g", 3, 0, 1, 2)
         m2fin(2, 0, 1)
         m1s(3, 2, 3)
         ycopy(3, 2, 3)
         qy(3, 0)
-        m2fin(2, 2, 3)
-        for h in range(2):
-            if h == 0:
-                qy(3, 1)
-            for m in range(4):
-                m2(3, m, 256 * h, 256 * h + 256)
-                fin(3, m, 256 * h, 256 * h + 256)
-                if m % 2 == 1:
-                    store(3, m - 1, m + 1, 256 * h, 256 * h + 256)
+        m2(2, 2, 0, N)
+        fin(2, 2, 0, N)
+        store(2, 2, 3, 0, N)
+        m2(2, 3, 0, N)
+        qy(3, 1)
+        fin(2, 3, 0, N)
+        store(2, 3, 4, 0, N)
+        m2(3, 3, 0, N)
+        fin_sg(3, 3)
+        for m in range(3):
+            m2(3, m, 0, N)
+            fin(3, m, 0, N)
+            store(3, m, m + 1, 0, N)
+        store(3, 3, 4, 0, N)

@@ -169,12 +169,12 @@ def tile_cnl_pb_w4_kernel(
                         op1=ADD,
                     )
 
-        def fin_sg(b, m):
-            scaled = keep.tile([P, N], F32, align_bytes=64, bufs=2)
+        def fin_sg(b, m, n0, n1):
+            scaled = keep.tile([P, n1 - n0], F32, align_bytes=64, bufs=2)
             nc.scalar.activation(
-                out=scaled[:], in_=zps[(b, m, 0)][:], func=IDENT, bias=bias[:, m : m + 1], scale=inv[:, m : m + 1]
+                out=scaled[:], in_=zps[(b, m, n0)][:], func=IDENT, bias=bias[:, m : m + 1], scale=inv[:, m : m + 1]
             )
-            nc.gpsimd.tensor_tensor(out=ot[b][:, m, :], in0=scaled[:], in1=xb[b][:, m, :], op=ADD)
+            nc.gpsimd.tensor_tensor(out=ot[b][:, m, n0:n1], in0=scaled[:], in1=xb[b][:, m, n0:n1], op=ADD)
 
         def widen_s(b, *planes):
             for t in planes:
@@ -208,6 +208,14 @@ def tile_cnl_pb_w4_kernel(
 
         def qy(b, h):
             quant(yi[b], yc[b], ys[b], 256 * h, 256 * h + 256)
+
+        zeros = keep.tile([P, N], BF16, align_bytes=64)
+        nc.vector.memset(zeros[:].bitcast(I32), 0)
+
+        def warm(k):
+            for i in range(k):
+                junk = psum.tile([P, N], F32, tag="zp", bufs=3)
+                nc.tensor.matmul(junk[:], lhsT=ident_bf[:], rhs=zeros[:], start=True, stop=True)
 
         xts = {}
 
@@ -291,9 +299,11 @@ def tile_cnl_pb_w4_kernel(
                 elif m % 2 == 1:
                     store(b, m - 1, m + 1, 0, N)
 
+        warm(4)
         widen_s(0, 0)
         widen_v(0, 1, 2, 3)
         params_turn()
+        warm(2)
         turn(0, 0)
         turn(0, 1)
         inter(0, 0)
@@ -339,12 +349,13 @@ def tile_cnl_pb_w4_kernel(
         widen_s(3, 0, 1, 2, 3)
         gate(2)
         addb("g", 2, 0, 1, 2, 3)
-        m2fin(1, 0, 1, 2, 3)
+        m2fin(1, 0, 1, 2)
+        qa(2)
+        m2fin(1, 3)
         turn(3, 0)
         turn(3, 1)
         acopy(3, 0)
         acopy(3, 1)
-        qa(2)
         inter(3, 0)
         m1s(2, 0, 1, 2, 3)
         ycopy(2, 0, 1, 2, 3)
@@ -370,7 +381,7 @@ def tile_cnl_pb_w4_kernel(
         fin(2, 3, 0, N)
         store(2, 3, 4, 0, N)
         m2(3, 3, 0, N)
-        fin_sg(3, 3)
+        fin_sg(3, 3, 0, N)
         for m in range(3):
             m2(3, m, 0, N)
             fin(3, m, 0, N)

from contextlib import ExitStack

import concourse.mybir as mybir
from concourse.masks import make_identity

F32 = mybir.dt.float32
BF16 = mybir.dt.bfloat16
I32 = mybir.dt.int32
U32 = mybir.dt.uint32
U8 = mybir.dt.uint8
FP8 = mybir.dt.float8_e4m3fn
FP8X4 = mybir.dt.float8_e4m3fn_x4
FP4X4 = mybir.dt.float4_e2m1fn_x4
ADD = mybir.AluOpType.add
SUB = mybir.AluOpType.subtract
MULT = mybir.AluOpType.mult
POW = mybir.AluOpType.pow
COPY = mybir.ActivationFunctionType.Copy
IDENT = mybir.ActivationFunctionType.Identity

P = 128
B = 4
C = 512
N = 512
EPS = 1e-5
FLOPS = 2 * (2 * B * C * C * N)


def tile_cnl_pb_w4_kernel(
    tc, attention, g_x_bytes, g_x_scale, x, Ww_words, Ww_scales, bw, gamma, beta, run_mean, run_var, out
):
    nc = tc.nc
    with ExitStack() as ctx:
        keep = ctx.enter_context(tc.tile_pool(name="keep", bufs=1))
        per = ctx.enter_context(tc.tile_pool(name="per", bufs=B))
        psum = ctx.enter_context(tc.psum_pool(name="psum", bufs=3))
        ctx.enter_context(tc.manual_schedule())

        ident = keep.tile([P, P], F32)
        make_identity(nc, ident[:])
        ws_raw = keep.tile([P, C], U8, align_bytes=64)
        rows = keep.tile([P, C], BF16, align_bytes=64)
        nc.vector.memset(rows[:].bitcast(I32), 0)
        nc.vector.memset(ws_raw[:].bitcast(I32), 0)
        gsc = keep.tile([P, 4], F32)

        gb, ab, xb = [], [], []
        for b in range(B):
            g_bytes = per.tile([P, 4, N], U8, align_bytes=64)
            gb.append(g_bytes)
            a_raw = per.tile([P, 4, C], BF16, align_bytes=64)
            ab.append(a_raw)
            x_raw = per.tile([P, 4, N], BF16, align_bytes=64)
            xb.append(x_raw)

        def load_g(b):
            nc.sync.dma_start(out=gb[b][:], in_=g_x_bytes[b].rearrange("(p t) n -> p t n", t=4))

        def load_a(b, t0, t1):
            nc.sync.dma_start(
                out=ab[b][:, t0:t1, :], in_=attention[b].rearrange("(p t) k -> p t k", t=4)[:, t0:t1, :]
            )

        def load_x(b):
            nc.sync.dma_start(out=xb[b][:], in_=x[b].rearrange("(m p) h w -> p m (h w)", m=4))

        w_raw = keep.tile([P, 2 * C], U8, align_bytes=64)
        load_g(0)
        load_a(0, 0, 4)
        nc.scalar.dma_start(out=gsc[:], in_=g_x_scale.rearrange("o (p t) u -> p (o t u)", t=4))
        for i, v in enumerate((run_var, gamma, bw, run_mean, beta)):
            nc.scalar.dma_start(out=rows[i : i + 1, :], in_=v.rearrange("(o c) -> o c", o=1))
        load_g(1)
        load_a(1, 0, 4)
        nc.sync.dma_start(out=w_raw[:], in_=Ww_words[0])
        load_x(0)
        for r in range(4):
            nc.sync.dma_start(
                out=ws_raw[32 * r : 32 * r + 4, :].bitcast(I32), in_=Ww_scales[0, 4 * r : 4 * r + 4, :].bitcast(I32)
            )
        load_g(2)
        load_a(2, 0, 4)
        load_x(1)
        load_g(3)
        load_a(3, 0, 4)
        load_x(2)
        load_x(3)

        negh = keep.tile([P, 4], F32)
        nc.gpsimd.memset(negh[:], -0.5)
        prm = keep.tile([P, 5, 4], F32)
        ve = keep.tile([P, 4], F32)
        inv = keep.tile([P, 4], F32)
        bias = keep.tile([P, 4], F32)
        rs = keep.tile([P, 4], F32)
        dm = keep.tile([P, 4], F32)
        de = keep.tile([P, 4], F32)
        ident_bf = keep.tile([P, P], BF16)
        nc.vector.tensor_copy(out=ident_bf[:], in_=ident[:])

        pts = []

        def params_turn():
            pt = psum.tile([P, 4, P], BF16, tag="zp", bufs=3)
            for m in range(4):
                nc.tensor.transpose(pt[:, m, :], rows[:, m * P : m * P + P], ident_bf[:])
            pts.append(pt)

        def params():
            pt = pts[0]
            nc.vector.tensor_copy(out=prm[:].rearrange("p i m -> p m i"), in_=pt[:, :, 0:5])
            nc.gpsimd.tensor_scalar(out=ve[:], in0=prm[:, 0, :], scalar1=EPS, scalar2=None, op0=ADD)
            nc.gpsimd.tensor_tensor(out=rs[:], in0=ve[:], in1=negh[:], op=POW)
            nc.gpsimd.tensor_tensor(out=inv[:], in0=rs[:], in1=prm[:, 1, :], op=MULT)
            nc.gpsimd.tensor_tensor(out=dm[:], in0=prm[:, 2, :], in1=prm[:, 3, :], op=SUB)
            nc.gpsimd.tensor_tensor(out=de[:], in0=dm[:], in1=inv[:], op=MULT)
            nc.gpsimd.tensor_tensor(out=bias[:], in0=de[:], in1=prm[:, 4, :], op=ADD)

        gp, gi, gc, gs, ai, ac, asc, yi, yc, ys, ot = ([] for i in range(11))
        xp = {}
        for b in range(B):
            g_planes = per.tile([P, 4, N], BF16, align_bytes=64)
            gp.append(g_planes)
            g_inter = per.tile([P, 4 * N], BF16, align_bytes=64)
            gi.append(g_inter)
            g_codes = per.tile([P, N], U32, align_bytes=64)
            gc.append(g_codes)
            g_scales = per.tile([P, N], U8, align_bytes=64)
            gs.append(g_scales)
            a_inter = per.tile([P, 4 * C], BF16, align_bytes=64)
            ai.append(a_inter)
            a_codes = per.tile([P, C], U32, align_bytes=64)
            ac.append(a_codes)
            a_scales = per.tile([P, C], U8, align_bytes=64)
            asc.append(a_scales)
            y_inter = per.tile([P, 4 * N], BF16, align_bytes=64)
            yi.append(y_inter)
            y_codes = per.tile([P, N], U32, align_bytes=64)
            yc.append(y_codes)
            y_scales = per.tile([P, N], U8, align_bytes=64)
            ys.append(y_scales)
            o_tile = per.tile([P, 4, N], F32, align_bytes=64)
            ot.append(o_tile)

        gates = {}

        def gate(b):
            gated = per.tile([P, 4], F32)
            nc.vector.tensor_copy(out=gated[:], in_=bias[:])
            gates[b] = gated

        def addb(engine, b, *ms):
            for m in ms:
                x_plus = keep.tile([P, N], F32, align_bytes=64, name="x_plus_%d_%d" % (b, m), tag="x_plus_%d" % m, bufs=2)
                xp[(b, m)] = x_plus
                if engine == "s":
                    nc.scalar.activation(out=x_plus[:], in_=xb[b][:, m, :], func=IDENT, bias=bias[:, m : m + 1])
                elif engine == "v":
                    nc.vector.tensor_scalar(
                        out=x_plus[:], in0=xb[b][:, m, :], scalar1=bias[:, m : m + 1], scalar2=None, op0=ADD
                    )
                else:
                    nc.gpsimd.tensor_scalar(
                        out=x_plus[:],
                        in0=xb[b][:, m, :],
                        scalar1=1.0,
                        scalar2=gates[b][:, m : m + 1],
                        op0=MULT,
                        op1=ADD,
                    )

        def fin_sg(b, m, n0, n1):
            scaled = keep.tile([P, n1 - n0], F32, align_bytes=64, bufs=2)
            nc.scalar.activation(
                out=scaled[:], in_=zps[(b, m, n0)][:], func=IDENT, bias=bias[:, m : m + 1], scale=inv[:, m : m + 1]
            )
            nc.gpsimd.tensor_tensor(out=ot[b][:, m, n0:n1], in0=scaled[:], in1=xb[b][:, m, n0:n1], op=ADD)

        def widen_s(b, *planes):
            for t in planes:
                nc.scalar.activation(
                    out=gp[b][:, t, :], in_=gb[b][:, t, :].bitcast(FP8), func=COPY, scale=gsc[:, t : t + 1]
                )

        def widen_v(b, *planes):
            for t in planes:
                nc.vector.tensor_scalar(
                    out=gp[b][:, t, :], in0=gb[b][:, t, :].bitcast(FP8), scalar1=gsc[:, t : t + 1], scalar2=None, op0=MULT
                )

        def inter(b, h):
            n0, n1 = h * 256, (h + 1) * 256
            nc.vector.tensor_copy(
                out=gi[b][:, 4 * n0 : 4 * n1].rearrange("p (c i t) -> p c t i", i=4, t=4),
                in_=gp[b][:, :, n0:n1].rearrange("p t (c i) -> p c t i", i=4),
            )

        def quant(src, codes, scales, c0, c1):
            nc.vector.quantize_mx(
                out=codes[:, c0:c1].bitcast(FP8X4), scales=scales[:, c0:c1], in_=src[:, 4 * c0 : 4 * c1]
            )

        def qg(b, c0, c1):
            quant(gi[b], gc[b], gs[b], c0, c1)

        def qa(b):
            quant(ai[b], ac[b], asc[b], 0, C)

        def qy(b, h):
            quant(yi[b], yc[b], ys[b], 256 * h, 256 * h + 256)

        zeros = keep.tile([P, N], BF16, align_bytes=64)
        nc.vector.memset(zeros[:].bitcast(I32), 0)

        def warm(k):
            for i in range(k):
                junk = psum.tile([P, N], F32, tag="zp", bufs=3)
                nc.tensor.matmul(junk[:], lhsT=ident_bf[:], rhs=zeros[:], start=True, stop=True)

        xts = {}

        def turn(b, h):
            xt = psum.tile([P, 2, 2, P], F32, bufs=2)
            for i in range(2):
                words = ab[b][:, 2 * h + i, :].bitcast(F32)
                for u in range(2):
                    nc.tensor.transpose(xt[:, i, u, :], words[:, u : C // 2 : 2], ident[:])
            xts[(b, h)] = xt

        def acopy(b, h):
            nc.scalar.copy(
                out=ai[b][:, 1024 * h : 1024 * h + 1024].bitcast(F32).rearrange("p (i m u) -> p i m u", i=2, u=2),
                in_=xts[(b, h)][:].rearrange("p i u m -> p i m u"),
            )

        yps = {}

        def m1(b, j):
            yp = psum.tile([P, 4, P], F32, bufs=3)
            for t in range(4):
                nc.tensor.matmul_mx(
                    out=yp[:, t, :],
                    lhsT=ac[b][:, t * P : t * P + P].bitcast(FP8X4),
                    lhsT_scale=asc[b][:, t * P : t * P + P],
                    rhs=gc[b][:, j * P : j * P + P].bitcast(FP8X4),
                    rhs_scale=gs[b][:, j * P : j * P + P],
                    start=True,
                    stop=True,
                )
            yps[(b, j)] = yp

        def ycopy(b, *js):
            for j in js:
                nc.scalar.copy(
                    out=yi[b][:, 512 * j : 512 * j + 512].rearrange("p (n t) -> p n t", t=4),
                    in_=yps[(b, j)][:].rearrange("p t n -> p n t"),
                )

        zps = {}

        def m2(b, m, n0, n1):
            zp = psum.tile([P, n1 - n0], F32, tag="zp", bufs=3)
            nc.tensor.matmul_mx(
                out=zp[:],
                lhsT=w_raw[:, 2 * P * m : 2 * P * m + 2 * P].bitcast(FP4X4),
                lhsT_scale=ws_raw[:, P * m : P * m + P],
                rhs=yc[b][:, n0:n1].bitcast(FP8X4),
                rhs_scale=ys[b][:, n0:n1],
                start=True,
                stop=True,
            )
            zps[(b, m, n0)] = zp

        def fin(b, m, n0, n1):
            nc.vector.scalar_tensor_tensor(
                out=ot[b][:, m, n0:n1],
                in0=zps[(b, m, n0)][:],
                scalar=inv[:, m : m + 1],
                in1=xp[(b, m)][:, n0:n1],
                op0=MULT,
                op1=ADD,
            )

        def store(b, m0, m1_, n0, n1):
            nc.sync.dma_start(
                out=out[b].rearrange("(m p) h w -> p m (h w)", m=4)[:, m0:m1_, n0:n1], in_=ot[b][:, m0:m1_, n0:n1]
            )

        def m1s(b, *js):
            for j in js:
                m1(b, j)

        def m2fin(b, *ms):
            for m in ms:
                m2(b, m, 0, N)
                fin(b, m, 0, N)
                if b >= 2:
                    store(b, m, m + 1, 0, N)
                elif m % 2 == 1:
                    store(b, m - 1, m + 1, 0, N)

        warm(4)
        widen_s(0, 0)
        widen_v(0, 1, 2, 3)
        params_turn()
        warm(2)
        turn(0, 0)
        turn(0, 1)
        inter(0, 0)
        acopy(0, 0)
        acopy(0, 1)
        inter(0, 1)
        params()
        qg(0, 0, 256)
        widen_v(1, 0, 1)
        qa(0)
        qg(0, 256, 512)
        turn(1, 0)
        turn(1, 1)
        widen_s(1, 2, 3)
        acopy(1, 0)
        acopy(1, 1)
        inter(1, 0)
        inter(1, 1)
        m1s(0, 0, 1, 2, 3)
        qa(1)
        ycopy(0, 0, 1, 2, 3)
        qy(0, 0)
        qg(1, 0, 512)
        qy(0, 1)
        m1s(1, 0, 1)
        addb("v", 0, 2, 3)
        addb("s", 0, 0, 1)
        gate(1)
        addb("g", 1, 0, 1, 2, 3)
        widen_s(2, 0, 1, 2, 3)
        m2fin(0, 0, 1, 2, 3)
        m1s(1, 2, 3)
        turn(2, 0)
        turn(2, 1)
        ycopy(1, 0, 1, 2, 3)
        inter(2, 0)
        qy(1, 0)
        inter(2, 1)
        qy(1, 1)
        qg(2, 0, 512)
        acopy(2, 0)
        acopy(2, 1)
        widen_s(3, 0, 1, 2, 3)
        gate(2)
        addb("g", 2, 0, 1, 2, 3)
        m2fin(1, 0, 1, 2)
        qa(2)
        m2fin(1, 3)
        turn(3, 0)
        turn(3, 1)
        acopy(3, 0)
        acopy(3, 1)
        inter(3, 0)
        m1s(2, 0, 1, 2, 3)
        ycopy(2, 0, 1, 2, 3)
        inter(3, 1)
        qa(3)
        qg(3, 0, 256)
        m1s(3, 0, 1)
        qy(2, 0)
        qy(2, 1)
        qg(3, 256, 512)
        ycopy(3, 0, 1)
        gate(3)
        addb("g", 3, 0, 1, 2)
        m2fin(2, 0, 1)
        m1s(3, 2, 3)
        ycopy(3, 2, 3)
        qy(3, 0)
        m2(2, 2, 0, N)
        fin(2, 2, 0, N)
        store(2, 2, 3, 0, N)
        m2(2, 3, 0, N)
        qy(3, 1)
        fin(2, 3, 0, N)
        store(2, 3, 4, 0, N)
        m2(3, 3, 0, N)
        fin_sg(3, 3, 0, N)
        for m in range(3):
            m2(3, m, 0, N)
            fin(3, m, 0, N)
            store(3, m, m + 1, 0, N)
        store(3, 3, 4, 0, N)
